import numpy as np
import ml_dtypes


BF16 = ml_dtypes.bfloat16


def bf(x):
    return np.asarray(x, np.float32).astype(BF16)


def f64(x):
    return np.asarray(x).astype(np.float64)


E2M1 = np.array([0.0, 0.5, 1.0, 1.5, 2.0, 3.0, 4.0, 6.0, -0.0, -0.5, -1.0, -1.5, -2.0, -3.0, -4.0, -6.0])


def pack_weight(w, fmt):
    k, n = w.shape
    w = f64(bf(w)).reshape(k // 32, 32, n)
    amax = np.abs(w).max(1)
    if fmt == "e4m3":
        byte = np.frexp(amax)[1] - 1 + 127 - 7
    else:
        mant, ex = np.frexp(amax / 6.0)
        byte = np.where(mant > 0.5, ex, ex - 1) + 127
    byte = np.clip(np.where(amax > 0, byte, 1), 1, 254)
    scaled = (w * np.exp2(127.0 - byte)[:, None, :]).reshape(k, n).astype(np.float32)
    by_word = np.ascontiguousarray(scaled.reshape(k // 512, 128, 4, n).transpose(0, 1, 3, 2))
    if fmt == "e4m3":
        words = by_word.astype(ml_dtypes.float8_e4m3fn).view(np.uint8)
    else:
        c = by_word.astype(ml_dtypes.float4_e2m1fn).view(np.uint8) & 0xF
        words = c[..., 0::2] | (c[..., 1::2] << 4)
    return np.ascontiguousarray(words), np.ascontiguousarray(byte.astype(np.uint8).reshape(k // 512, 16, n))


def unpack_weight(words, scales, fmt):
    g, p, n, _ = words.shape
    if fmt == "e4m3":
        vals = np.ascontiguousarray(words).view(ml_dtypes.float8_e4m3fn).astype(np.float64)
    else:
        nib = np.empty((g, p, n, 4), np.uint8)
        nib[..., 0::2] = words & 0xF
        nib[..., 1::2] = words >> 4
        vals = E2M1[nib]
    vals = vals * np.repeat(np.exp2(scales.astype(np.float64) - 127.0), 8, axis=1)[..., None]
    return vals.transpose(0, 1, 3, 2).reshape(g * 512, n)

def pack4(w):
    words, scales = pack_weight(w, "e2m1")
    return words.reshape(words.shape[0], 128, -1), scales


def unpack4(words, scales):
    return unpack_weight(words.reshape(words.shape[0], 128, -1, 2), scales, "e2m1")


def kspread(k):
    return np.exp2(np.repeat(np.random.randint(-6, 7, k // 32), 32).astype(np.float64))


B, S, H, D = 4, 128, 16, 256
T = B * S
HID = H * D
D2 = D // 2
ROPE_THETA = 10000.0


def rotary(x, cos, sin):
    x1, x2 = x[..., :D2], x[..., D2:]
    c, s = cos[:, None, :], sin[:, None, :]
    return np.concatenate([x1 * c - x2 * s, x2 * c + x1 * s], axis=-1)


def setup_inputs():
    s = kspread(HID)
    pos = np.tile(np.arange(S, dtype=np.float64), B)
    inv_freq = 1.0 / ROPE_THETA ** (np.arange(0, D, 2, dtype=np.float64) / D)
    freqs = pos[:, None] * inv_freq[None, :]
    hidden_states = np.random.standard_normal((T, HID)) * s
    hidden_states_words, hidden_states_scales = pack4(np.ascontiguousarray(hidden_states.T))
    w = np.random.standard_normal((3 * HID, HID)) / np.sqrt(HID) / s[None, :]
    words, scales = pack4(np.ascontiguousarray(w.T))
    b_qkv = bf(np.random.standard_normal(3 * HID) * 0.3)
    return {"hidden_states_words": hidden_states_words,
            "hidden_states_scales": hidden_states_scales,
            "cos": bf(np.cos(freqs)),
            "sin": bf(np.sin(freqs)),
            "w_qkv_words": words,
            "w_qkv_scales": scales,
            "b_qkv": b_qkv}


def reference(hidden_states_words, hidden_states_scales, cos, sin, w_qkv_words, w_qkv_scales, b_qkv):
    proj = unpack4(hidden_states_words, hidden_states_scales).T @ unpack4(w_qkv_words, w_qkv_scales)
    qkv = (proj + f64(b_qkv)).reshape(T, 3, H, D)
    q = rotary(qkv[:, 0], f64(cos), f64(sin))
    k = rotary(qkv[:, 1], f64(cos), f64(sin))
    v = qkv[:, 2]
    return q, k, v

@@ -1,0 +1,226 @@
+from contextlib import ExitStack
+
+import concourse.mybir as mybir
+
+FLOPS = 2 * 512 * 4096 * 12288
+
+F32 = mybir.dt.float32
+BF16 = mybir.dt.bfloat16
+U8 = mybir.dt.uint8
+I32 = mybir.dt.int32
+FP4X4 = mybir.dt.float4_e2m1fn_x4
+ADD = mybir.AluOpType.add
+SUB = mybir.AluOpType.subtract
+MULT = mybir.AluOpType.mult
+
+P = 128
+PASSES = 8
+TOK_TILES = 4
+BLK = 512
+UNIT = 1024
+SLOTS = 6
+PART_COLS = 4096
+Q_PART, K_PART, V_PART = 0, 1, 2
+
+
+def tile_flashneoxattention_pa_kernel(
+    tc, x_words, x_scales, cos, sin, w_words, w_scales, b_qkv, out_q, out_k, out_v
+):
+    nc = tc.nc
+    outs = [o.rearrange("t h d -> t (h d)") for o in (out_q, out_k, out_v)]
+
+    units = []
+    for a in range(4):
+        units.extend([(V_PART, a), (Q_PART, a), (K_PART, a)])
+    unit_index = dict((u, i) for i, u in enumerate(units))
+
+    v_after = {(0, 0): (1, 0), (0, 1): (1, 1), (1, 0): (2, 0), (1, 1): (2, 1), (2, 1): (3, 0), (3, 1): (3, 1)}
+    blocks = []
+    for a in range(4):
+        for half in range(2):
+            blocks.append((Q_PART, a, half))
+            blocks.append((K_PART, a, half))
+            if (a, half) in v_after:
+                va, vh = v_after[(a, half)]
+                blocks.append((V_PART, va, vh))
+
+    with ExitStack() as ctx:
+        keep = ctx.enter_context(tc.tile_pool(name="keep", bufs=1))
+        work = ctx.enter_context(tc.tile_pool(name="work", bufs=3))
+        psum = ctx.enter_context(tc.psum_pool(name="psum", bufs=8))
+        ctx.enter_context(tc.manual_schedule())
+
+        x_codes = keep.tile([P, PASSES, 2 * 512], U8, name="x_codes", align_bytes=64)
+        x_planes = keep.tile([P, PASSES, 512], U8, name="x_planes", align_bytes=64)
+        w_codes = [keep.tile([P, PASSES, 2 * UNIT], U8, name="w_codes%d" % s, align_bytes=64) for s in range(SLOTS)]
+        w_planes = [keep.tile([P, PASSES, UNIT], U8, name="w_planes%d" % s, align_bytes=64) for s in range(SLOTS)]
+        bias = keep.tile([P, 3 * PART_COLS], BF16, name="bias")
+        cos_sb = keep.tile([P, TOK_TILES, 128], BF16, name="cos_sb")
+        sin_sb = keep.tile([P, TOK_TILES, 128], BF16, name="sin_sb")
+
+        def unit_col0(u):
+            return units[u][0] * PART_COLS + units[u][1] * UNIT
+
+        def zero(plane, g0, g1):
+            nc.vector.memset(plane[:, g0:g1, :].bitcast(I32), 0)
+
+        def load_x_codes(g0, g1):
+            nc.sync.dma_start(
+                out=x_codes[:, g0:g1, :].bitcast(I32),
+                in_=x_words[g0:g1].rearrange("g p b -> p g b").bitcast(I32),
+            )
+
+        def load_x_scales(g0, g1):
+            for quad in range(4):
+                nc.sync.dma_start(
+                    out=x_planes[32 * quad : 32 * quad + 4, g0:g1, :].bitcast(I32),
+                    in_=x_scales[g0:g1, 4 * quad : 4 * quad + 4, :].rearrange("g r n -> r g n").bitcast(I32),
+                )
+
+        def load_w_codes(u, g0, g1, c0, c1):
+            col = unit_col0(u)
+            nc.sync.dma_start(
+                out=w_codes[u % SLOTS][:, g0:g1, 2 * c0 : 2 * c1].bitcast(I32),
+                in_=w_words[g0:g1, :, 2 * (col + c0) : 2 * (col + c1)].rearrange("g p b -> p g b").bitcast(I32),
+            )
+
+        def load_w_scales(u, g0, g1, c0, c1):
+            col = unit_col0(u)
+            for quad in range(4):
+                nc.sync.dma_start(
+                    out=w_planes[u % SLOTS][32 * quad : 32 * quad + 4, g0:g1, c0:c1].bitcast(I32),
+                    in_=w_scales[g0:g1, 4 * quad : 4 * quad + 4, col + c0 : col + c1]
+                    .rearrange("g r n -> r g n")
+                    .bitcast(I32),
+                )
+
+        def load_bias(u):
+            col = unit_col0(u)
+            nc.sync.dma_start(out=bias[:, col : col + UNIT], in_=b_qkv[col : col + UNIT].partition_broadcast(P))
+
+        def load_unit(u):
+            load_w_scales(u, 0, PASSES, 0, UNIT)
+            load_w_codes(u, 0, PASSES, 0, UNIT)
+            load_bias(u)
+
+        def multiply(acc, u, half, m, g):
+            slot = u % SLOTS
+            nc.tensor.matmul_mx(
+                out=acc[:],
+                lhsT=x_codes[:, g, 256 * m : 256 * (m + 1)].bitcast(FP4X4),
+                lhsT_scale=x_planes[:, g, 128 * m : 128 * (m + 1)],
+                rhs=w_codes[slot][:, g, 2 * BLK * half : 2 * BLK * (half + 1)].bitcast(FP4X4),
+                rhs_scale=w_planes[slot][:, g, BLK * half : BLK * (half + 1)],
+                start=(g == 0),
+                stop=(g == PASSES - 1),
+            )
+
+        def store(res, part, a, half, m):
+            c0 = a * UNIT + half * BLK
+            nc.scalar.dma_start(out=outs[part][P * m : P * (m + 1), c0 : c0 + BLK], in_=res[:])
+
+        def add_bias(dst, acc, part, a, half):
+            col = part * PART_COLS + a * UNIT + half * BLK
+            nc.vector.tensor_tensor(out=dst[:], in0=acc[:], in1=bias[:, col : col + BLK], op=ADD)
+
+        def value_bank(acc, a, half, m):
+            res = work.tile([P, BLK], F32, name="res", bufs=6)
+            add_bias(res, acc, V_PART, a, half)
+            store(res, V_PART, a, half, m)
+
+        def products(y, m):
+            yc = work.tile([P, 4, 128], F32, name="yc")
+            ys = work.tile([P, 4, 128], F32, name="ys")
+            y3 = y[:].rearrange("p (a d) -> p a d", d=128)
+            nc.vector.tensor_tensor(
+                out=yc[:], in0=y3, in1=cos_sb[:, m, :].unsqueeze(1).to_broadcast([P, 4, 128]), op=MULT
+            )
+            nc.vector.tensor_tensor(
+                out=ys[:], in0=y3, in1=sin_sb[:, m, :].unsqueeze(1).to_broadcast([P, 4, 128]), op=MULT
+            )
+            return yc, ys
+
+        def combine(yc, ys, part, a, half, m):
+            res = work.tile([P, BLK], F32, name="res", bufs=6)
+            r4 = res[:].rearrange("p (h j d) -> p h j d", j=2, d=128)
+            c4 = yc[:].rearrange("p (h j) d -> p h j d", j=2)
+            s4 = ys[:].rearrange("p (h j) d -> p h j d", j=2)
+            nc.vector.tensor_tensor(out=r4[:, :, 0, :], in0=c4[:, :, 0, :], in1=s4[:, :, 1, :], op=SUB)
+            nc.vector.tensor_tensor(out=r4[:, :, 1, :], in0=c4[:, :, 1, :], in1=s4[:, :, 0, :], op=ADD)
+            store(res, part, a, half, m)
+
+        zero(x_planes, 0, 2)
+        zero(w_planes[0], 0, 2)
+        zero(x_planes, 2, PASSES)
+        zero(w_planes[0], 2, PASSES)
+        for s in range(1, SLOTS):
+            zero(w_planes[s], 0, PASSES)
+
+        load_x_codes(0, 1)
+        load_w_codes(0, 0, 1, 0, UNIT)
+        load_x_scales(0, 2)
+        load_w_scales(0, 0, 2, 0, UNIT)
+        load_x_codes(1, 2)
+        load_w_codes(0, 1, 2, 0, UNIT)
+        load_x_scales(2, 4)
+        load_w_scales(0, 2, 4, 0, UNIT)
+        load_x_codes(2, 4)
+        load_w_codes(0, 2, 4, 0, UNIT)
+        load_x_scales(4, PASSES)
+        load_w_scales(0, 4, PASSES, 0, UNIT)
+        load_x_codes(4, 6)
+        load_w_codes(0, 4, 6, 0, UNIT)
+        load_x_codes(6, PASSES)
+        load_w_codes(0, 6, PASSES, 0, UNIT)
+        load_bias(0)
+        for half in range(2):
+            for u in (1, 2, 3):
+                load_w_scales(u, 0, PASSES, BLK * half, BLK * (half + 1))
+                load_w_codes(u, 0, PASSES, BLK * half, BLK * (half + 1))
+                if half == 0:
+                    if u == 1:
+                        nc.sync.dma_start(out=cos_sb[:], in_=cos.rearrange("(m p) d -> p m d", p=P))
+                        nc.sync.dma_start(out=sin_sb[:], in_=sin.rearrange("(m p) d -> p m d", p=P))
+                    load_bias(u)
+        load_unit(4)
+        load_unit(5)
+        next_unit = SLOTS
+        uses_left = [2] * len(units)
+
+        head = [psum.tile([P, BLK], F32, name="acc") for i in range(8)]
+        for g in range(PASSES):
+            for half in range(2):
+                for m in range(TOK_TILES):
+                    multiply(head[4 * half + m], 0, half, m, g)
+        for half in range(2):
+            for m in range(TOK_TILES):
+                value_bank(head[4 * half + m], 0, half, m)
+        uses_left[0] = 0
+        load_unit(next_unit)
+        next_unit += 1
+
+        pending = None
+        for part, a, half in blocks:
+            u = unit_index[(part, a)]
+            for m in range(TOK_TILES):
+                acc = psum.tile([P, BLK], F32, name="acc")
+                for g in range(PASSES):
+                    multiply(acc, u, half, m, g)
+                if part == V_PART:
+                    value_bank(acc, a, half, m)
+                    if pending is not None:
+                        combine(*pending)
+                        pending = None
+                else:
+                    y = work.tile([P, BLK], F32, name="y")
+                    add_bias(y, acc, part, a, half)
+                    if pending is not None:
+                        combine(*pending)
+                    yc, ys = products(y, m)
+                    pending = (yc, ys, part, a, half, m)
+            uses_left[u] -= 1
+            while next_unit < len(units) and uses_left[next_unit - SLOTS] == 0:
+                load_unit(next_unit)
+                next_unit += 1
+        if pending is not None:
+            combine(*pending)

@@ -18,7 +18,9 @@ PASSES = 8
 TOK_TILES = 4
 BLK = 512
 UNIT = 1024
-SLOTS = 6
+SLOTS = 4
+BANKS = 8
+WARM_MATMULS = 12
 PART_COLS = 4096
 Q_PART, K_PART, V_PART = 0, 1, 2
 
@@ -32,22 +34,13 @@ def tile_flashneoxattention_pa_kernel(
     units = []
     for a in range(4):
         units.extend([(V_PART, a), (Q_PART, a), (K_PART, a)])
-    unit_index = dict((u, i) for i, u in enumerate(units))
 
-    v_after = {(0, 0): (1, 0), (0, 1): (1, 1), (1, 0): (2, 0), (1, 1): (2, 1), (2, 1): (3, 0), (3, 1): (3, 1)}
-    blocks = []
-    for a in range(4):
-        for half in range(2):
-            blocks.append((Q_PART, a, half))
-            blocks.append((K_PART, a, half))
-            if (a, half) in v_after:
-                va, vh = v_after[(a, half)]
-                blocks.append((V_PART, va, vh))
+    steps = [(u, (0, 1)) for u in range(1, 9)] + [(9, (0,)), (10, (0, 1)), (11, (0, 1)), (9, (1,))]
 
     with ExitStack() as ctx:
         keep = ctx.enter_context(tc.tile_pool(name="keep", bufs=1))
-        work = ctx.enter_context(tc.tile_pool(name="work", bufs=3))
-        psum = ctx.enter_context(tc.psum_pool(name="psum", bufs=8))
+        work = ctx.enter_context(tc.tile_pool(name="work", bufs=2))
+        psum = ctx.enter_context(tc.psum_pool(name="psum", bufs=1))
         ctx.enter_context(tc.manual_schedule())
 
         x_codes = keep.tile([P, PASSES, 2 * 512], U8, name="x_codes", align_bytes=64)
@@ -77,19 +70,19 @@ def tile_flashneoxattention_pa_kernel(
                     in_=x_scales[g0:g1, 4 * quad : 4 * quad + 4, :].rearrange("g r n -> r g n").bitcast(I32),
                 )
 
-        def load_w_codes(u, g0, g1, c0, c1):
+        def load_w_codes(u, g0, g1):
             col = unit_col0(u)
             nc.sync.dma_start(
-                out=w_codes[u % SLOTS][:, g0:g1, 2 * c0 : 2 * c1].bitcast(I32),
-                in_=w_words[g0:g1, :, 2 * (col + c0) : 2 * (col + c1)].rearrange("g p b -> p g b").bitcast(I32),
+                out=w_codes[u % SLOTS][:, g0:g1, :].bitcast(I32),
+                in_=w_words[g0:g1, :, 2 * col : 2 * (col + UNIT)].rearrange("g p b -> p g b").bitcast(I32),
             )
 
-        def load_w_scales(u, g0, g1, c0, c1):
+        def load_w_scales(u, g0, g1):
             col = unit_col0(u)
             for quad in range(4):
                 nc.sync.dma_start(
-                    out=w_planes[u % SLOTS][32 * quad : 32 * quad + 4, g0:g1, c0:c1].bitcast(I32),
-                    in_=w_scales[g0:g1, 4 * quad : 4 * quad + 4, col + c0 : col + c1]
+                    out=w_planes[u % SLOTS][32 * quad : 32 * quad + 4, g0:g1, :].bitcast(I32),
+                    in_=w_scales[g0:g1, 4 * quad : 4 * quad + 4, col : col + UNIT]
                     .rearrange("g r n -> r g n")
                     .bitcast(I32),
                 )
@@ -99,128 +92,159 @@ def tile_flashneoxattention_pa_kernel(
             nc.sync.dma_start(out=bias[:, col : col + UNIT], in_=b_qkv[col : col + UNIT].partition_broadcast(P))
 
         def load_unit(u):
-            load_w_scales(u, 0, PASSES, 0, UNIT)
-            load_w_codes(u, 0, PASSES, 0, UNIT)
+            load_w_scales(u, 0, PASSES)
+            load_w_codes(u, 0, PASSES)
             load_bias(u)
 
-        def multiply(acc, u, half, m, g):
+        bank_count = [0]
+
+        def new_bank():
+            n = bank_count[0]
+            bank_count[0] = n + 1
+            return psum.tile([P, BLK], F32, name="acc%d" % (n % BANKS))
+
+        def multiply(acc, u, half, m, g, c0=0, width=BLK):
             slot = u % SLOTS
+            lo = BLK * half + c0
             nc.tensor.matmul_mx(
-                out=acc[:],
+                out=acc[:, 0:width],
                 lhsT=x_codes[:, g, 256 * m : 256 * (m + 1)].bitcast(FP4X4),
                 lhsT_scale=x_planes[:, g, 128 * m : 128 * (m + 1)],
-                rhs=w_codes[slot][:, g, 2 * BLK * half : 2 * BLK * (half + 1)].bitcast(FP4X4),
-                rhs_scale=w_planes[slot][:, g, BLK * half : BLK * (half + 1)],
+                rhs=w_codes[slot][:, g, 2 * lo : 2 * (lo + width)].bitcast(FP4X4),
+                rhs_scale=w_planes[slot][:, g, lo : lo + width],
                 start=(g == 0),
                 stop=(g == PASSES - 1),
             )
 
-        def store(res, part, a, half, m):
-            c0 = a * UNIT + half * BLK
-            nc.scalar.dma_start(out=outs[part][P * m : P * (m + 1), c0 : c0 + BLK], in_=res[:])
+        def add_bias(dst, accs, u, halves):
+            for i, half in enumerate(halves):
+                col = unit_col0(u) + half * BLK
+                nc.vector.tensor_tensor(
+                    out=dst[:, BLK * i : BLK * (i + 1)], in0=accs[i][:], in1=bias[:, col : col + BLK], op=ADD
+                )
 
-        def add_bias(dst, acc, part, a, half):
-            col = part * PART_COLS + a * UNIT + half * BLK
-            nc.vector.tensor_tensor(out=dst[:], in0=acc[:], in1=bias[:, col : col + BLK], op=ADD)
-
-        def value_bank(acc, a, half, m):
-            res = work.tile([P, BLK], F32, name="res", bufs=6)
-            add_bias(res, acc, V_PART, a, half)
-            store(res, V_PART, a, half, m)
+        def store(res, u, halves, m):
+            part, a = units[u]
+            c0 = a * UNIT + halves[0] * BLK
+            width = BLK * len(halves)
+            nc.scalar.dma_start(out=outs[part][P * m : P * (m + 1), c0 : c0 + width], in_=res[:, 0:width])
 
         def products(y, m):
-            yc = work.tile([P, 4, 128], F32, name="yc")
-            ys = work.tile([P, 4, 128], F32, name="ys")
+            yc = work.tile([P, 8, 128], F32, name="yc")
+            ys = work.tile([P, 8, 128], F32, name="ys")
             y3 = y[:].rearrange("p (a d) -> p a d", d=128)
             nc.vector.tensor_tensor(
-                out=yc[:], in0=y3, in1=cos_sb[:, m, :].unsqueeze(1).to_broadcast([P, 4, 128]), op=MULT
+                out=yc[:], in0=y3, in1=cos_sb[:, m, :].unsqueeze(1).to_broadcast([P, 8, 128]), op=MULT
             )
             nc.vector.tensor_tensor(
-                out=ys[:], in0=y3, in1=sin_sb[:, m, :].unsqueeze(1).to_broadcast([P, 4, 128]), op=MULT
+                out=ys[:], in0=y3, in1=sin_sb[:, m, :].unsqueeze(1).to_broadcast([P, 8, 128]), op=MULT
             )
             return yc, ys
 
-        def combine(yc, ys, part, a, half, m):
-            res = work.tile([P, BLK], F32, name="res", bufs=6)
+        def combine(yc, ys, u, halves, m):
+            res = work.tile([P, UNIT], F32, name="res", bufs=6)
             r4 = res[:].rearrange("p (h j d) -> p h j d", j=2, d=128)
             c4 = yc[:].rearrange("p (h j) d -> p h j d", j=2)
             s4 = ys[:].rearrange("p (h j) d -> p h j d", j=2)
             nc.vector.tensor_tensor(out=r4[:, :, 0, :], in0=c4[:, :, 0, :], in1=s4[:, :, 1, :], op=SUB)
             nc.vector.tensor_tensor(out=r4[:, :, 1, :], in0=c4[:, :, 1, :], in1=s4[:, :, 0, :], op=ADD)
-            store(res, part, a, half, m)
+            store(res, u, halves, m)
+
+        def value_rows(accs, u, halves, m):
+            res = work.tile([P, UNIT], F32, name="res", bufs=6)
+            add_bias(res, accs, u, halves)
+            store(res, u, halves, m)
+
+        warm = keep.tile([P, BLK], BF16, name="warm")
+        nc.gpsimd.memset(warm[:], 0.0)
+        warm_acc = psum.tile([P, BLK], F32, name="acc%d" % (BANKS - 1))
+        for i in range(WARM_MATMULS):
+            nc.tensor.matmul(out=warm_acc[:], lhsT=warm[:, 0:P], rhs=warm[:], start=True, stop=True)
 
         zero(x_planes, 0, 2)
         zero(w_planes[0], 0, 2)
         zero(x_planes, 2, PASSES)
         zero(w_planes[0], 2, PASSES)
-        for s in range(1, SLOTS):
-            zero(w_planes[s], 0, PASSES)
+        zero(w_planes[1], 0, PASSES)
+        zero(w_planes[2], 0, PASSES)
 
         load_x_codes(0, 1)
-        load_w_codes(0, 0, 1, 0, UNIT)
+        load_w_codes(0, 0, 1)
         load_x_scales(0, 2)
-        load_w_scales(0, 0, 2, 0, UNIT)
+        load_w_scales(0, 0, 2)
         load_x_codes(1, 2)
-        load_w_codes(0, 1, 2, 0, UNIT)
+        load_w_codes(0, 1, 2)
         load_x_scales(2, 4)
-        load_w_scales(0, 2, 4, 0, UNIT)
+        load_w_scales(0, 2, 4)
         load_x_codes(2, 4)
-        load_w_codes(0, 2, 4, 0, UNIT)
+        load_w_codes(0, 2, 4)
         load_x_scales(4, PASSES)
-        load_w_scales(0, 4, PASSES, 0, UNIT)
+        load_w_scales(0, 4, PASSES)
         load_x_codes(4, 6)
-        load_w_codes(0, 4, 6, 0, UNIT)
+        load_w_codes(0, 4, 6)
         load_x_codes(6, PASSES)
-        load_w_codes(0, 6, PASSES, 0, UNIT)
+        load_w_codes(0, 6, PASSES)
         load_bias(0)
-        for half in range(2):
-            for u in (1, 2, 3):
-                load_w_scales(u, 0, PASSES, BLK * half, BLK * (half + 1))
-                load_w_codes(u, 0, PASSES, BLK * half, BLK * (half + 1))
-                if half == 0:
-                    if u == 1:
-                        nc.sync.dma_start(out=cos_sb[:], in_=cos.rearrange("(m p) d -> p m d", p=P))
-                        nc.sync.dma_start(out=sin_sb[:], in_=sin.rearrange("(m p) d -> p m d", p=P))
-                    load_bias(u)
-        load_unit(4)
-        load_unit(5)
-        next_unit = SLOTS
-        uses_left = [2] * len(units)
+        load_w_scales(1, 0, PASSES)
+        load_w_codes(1, 0, PASSES)
+        nc.sync.dma_start(out=cos_sb[:], in_=cos.rearrange("(m p) d -> p m d", p=P))
+        nc.sync.dma_start(out=sin_sb[:], in_=sin.rearrange("(m p) d -> p m d", p=P))
+        load_bias(1)
+        load_unit(2)
 
-        head = [psum.tile([P, BLK], F32, name="acc") for i in range(8)]
+        head = [new_bank() for i in range(BANKS)]
         for g in range(PASSES):
-            for half in range(2):
-                for m in range(TOK_TILES):
-                    multiply(head[4 * half + m], 0, half, m, g)
-        for half in range(2):
             for m in range(TOK_TILES):
-                value_bank(head[4 * half + m], 0, half, m)
-        uses_left[0] = 0
-        load_unit(next_unit)
-        next_unit += 1
+                for half in range(2):
+                    multiply(head[2 * m + half], 0, half, m, g)
+        for m in range(TOK_TILES):
+            value_rows(head[2 * m : 2 * m + 2], 0, (0, 1), m)
+        zero(w_planes[3], 0, PASSES)
+        load_unit(3)
+        load_unit(4)
+        next_unit = 5
+        halves_left = [2] * len(units)
+        halves_left[0] = 0
 
         pending = None
-        for part, a, half in blocks:
-            u = unit_index[(part, a)]
+        for u, halves in steps:
+            last_step = (u, halves) == steps[-1]
             for m in range(TOK_TILES):
-                acc = psum.tile([P, BLK], F32, name="acc")
-                for g in range(PASSES):
-                    multiply(acc, u, half, m, g)
-                if part == V_PART:
-                    value_bank(acc, a, half, m)
+                if last_step and m == TOK_TILES - 1:
+                    break
+                accs = []
+                for half in halves:
+                    acc = new_bank()
+                    for g in range(PASSES):
+                        multiply(acc, u, half, m, g)
+                    accs.append(acc)
+                if units[u][0] == V_PART:
+                    value_rows(accs, u, halves, m)
                     if pending is not None:
                         combine(*pending)
                         pending = None
                 else:
-                    y = work.tile([P, BLK], F32, name="y")
-                    add_bias(y, acc, part, a, half)
+                    y = work.tile([P, UNIT], F32, name="y")
+                    add_bias(y, accs, u, halves)
                     if pending is not None:
                         combine(*pending)
                     yc, ys = products(y, m)
-                    pending = (yc, ys, part, a, half, m)
-            uses_left[u] -= 1
-            while next_unit < len(units) and uses_left[next_unit - SLOTS] == 0:
+                    pending = (yc, ys, u, halves, m)
+            halves_left[u] -= len(halves)
+            while next_unit < len(units) and halves_left[next_unit - SLOTS] == 0:
                 load_unit(next_unit)
                 next_unit += 1
-        if pending is not None:
-            combine(*pending)
+        u, halves = steps[-1]
+        m = TOK_TILES - 1
+        for i, queue in enumerate((nc.scalar, nc.sync)):
+            c0 = i * (BLK // 2)
+            acc = new_bank()
+            for g in range(PASSES):
+                multiply(acc, u, halves[0], m, g, c0, BLK // 2)
+            res = work.tile([P, UNIT], F32, name="res", bufs=6)
+            col = unit_col0(u) + halves[0] * BLK + c0
+            nc.vector.tensor_tensor(
+                out=res[:, 0 : BLK // 2], in0=acc[:, 0 : BLK // 2], in1=bias[:, col : col + BLK // 2], op=ADD
+            )
+            oc = units[u][1] * UNIT + halves[0] * BLK + c0
+            queue.dma_start(out=outs[V_PART][P * m : P * (m + 1), oc : oc + BLK // 2], in_=res[:, 0 : BLK // 2])

@@ -47,7 +47,7 @@ def tile_flashneoxattention_pa_kernel(
         x_planes = keep.tile([P, PASSES, 512], U8, name="x_planes", align_bytes=64)
         w_codes = [keep.tile([P, PASSES, 2 * UNIT], U8, name="w_codes%d" % s, align_bytes=64) for s in range(SLOTS)]
         w_planes = [keep.tile([P, PASSES, UNIT], U8, name="w_planes%d" % s, align_bytes=64) for s in range(SLOTS)]
-        bias = keep.tile([P, 3 * PART_COLS], BF16, name="bias")
+        bias = [keep.tile([P, UNIT], BF16, name="bias%d" % s) for s in range(SLOTS)]
         cos_sb = keep.tile([P, TOK_TILES, 128], BF16, name="cos_sb")
         sin_sb = keep.tile([P, TOK_TILES, 128], BF16, name="sin_sb")
 
@@ -89,7 +89,7 @@ def tile_flashneoxattention_pa_kernel(
 
         def load_bias(u):
             col = unit_col0(u)
-            nc.sync.dma_start(out=bias[:, col : col + UNIT], in_=b_qkv[col : col + UNIT].partition_broadcast(P))
+            nc.gpsimd.dma_start(out=bias[u % SLOTS][:], in_=b_qkv[col : col + UNIT].partition_broadcast(P))
 
         def load_unit(u):
             load_w_scales(u, 0, PASSES)
@@ -118,9 +118,11 @@ def tile_flashneoxattention_pa_kernel(
 
         def add_bias(dst, accs, u, halves):
             for i, half in enumerate(halves):
-                col = unit_col0(u) + half * BLK
                 nc.vector.tensor_tensor(
-                    out=dst[:, BLK * i : BLK * (i + 1)], in0=accs[i][:], in1=bias[:, col : col + BLK], op=ADD
+                    out=dst[:, BLK * i : BLK * (i + 1)],
+                    in0=accs[i][:],
+                    in1=bias[u % SLOTS][:, BLK * half : BLK * (half + 1)],
+                    op=ADD,
                 )
 
         def store(res, u, halves, m):
@@ -187,8 +189,8 @@ def tile_flashneoxattention_pa_kernel(
         load_bias(0)
         load_w_scales(1, 0, PASSES)
         load_w_codes(1, 0, PASSES)
-        nc.sync.dma_start(out=cos_sb[:], in_=cos.rearrange("(m p) d -> p m d", p=P))
-        nc.sync.dma_start(out=sin_sb[:], in_=sin.rearrange("(m p) d -> p m d", p=P))
+        nc.gpsimd.dma_start(out=cos_sb[:], in_=cos.rearrange("(m p) d -> p m d", p=P))
+        nc.gpsimd.dma_start(out=sin_sb[:], in_=sin.rearrange("(m p) d -> p m d", p=P))
         load_bias(1)
         load_unit(2)
 
@@ -242,9 +244,9 @@ def tile_flashneoxattention_pa_kernel(
             for g in range(PASSES):
                 multiply(acc, u, halves[0], m, g, c0, BLK // 2)
             res = work.tile([P, UNIT], F32, name="res", bufs=6)
-            col = unit_col0(u) + halves[0] * BLK + c0
+            col = halves[0] * BLK + c0
             nc.vector.tensor_tensor(
-                out=res[:, 0 : BLK // 2], in0=acc[:, 0 : BLK // 2], in1=bias[:, col : col + BLK // 2], op=ADD
+                out=res[:, 0 : BLK // 2], in0=acc[:, 0 : BLK // 2], in1=bias[u % SLOTS][:, col : col + BLK // 2], op=ADD
             )
             oc = units[u][1] * UNIT + halves[0] * BLK + c0
             queue.dma_start(out=outs[V_PART][P * m : P * (m + 1), oc : oc + BLK // 2], in_=res[:, 0 : BLK // 2])

@@ -47,7 +47,7 @@ def tile_flashneoxattention_pa_kernel(
         x_planes = keep.tile([P, PASSES, 512], U8, name="x_planes", align_bytes=64)
         w_codes = [keep.tile([P, PASSES, 2 * UNIT], U8, name="w_codes%d" % s, align_bytes=64) for s in range(SLOTS)]
         w_planes = [keep.tile([P, PASSES, UNIT], U8, name="w_planes%d" % s, align_bytes=64) for s in range(SLOTS)]
-        bias = [keep.tile([P, UNIT], BF16, name="bias%d" % s) for s in range(SLOTS)]
+        bias = keep.tile([P, 3 * PART_COLS], BF16, name="bias")
         cos_sb = keep.tile([P, TOK_TILES, 128], BF16, name="cos_sb")
         sin_sb = keep.tile([P, TOK_TILES, 128], BF16, name="sin_sb")
 
@@ -89,7 +89,7 @@ def tile_flashneoxattention_pa_kernel(
 
         def load_bias(u):
             col = unit_col0(u)
-            nc.gpsimd.dma_start(out=bias[u % SLOTS][:], in_=b_qkv[col : col + UNIT].partition_broadcast(P))
+            nc.sync.dma_start(out=bias[:, col : col + UNIT], in_=b_qkv[col : col + UNIT].partition_broadcast(P))
 
         def load_unit(u):
             load_w_scales(u, 0, PASSES)
@@ -117,19 +117,18 @@ def tile_flashneoxattention_pa_kernel(
             )
 
         def add_bias(dst, accs, u, halves):
-            for i, half in enumerate(halves):
-                nc.vector.tensor_tensor(
-                    out=dst[:, BLK * i : BLK * (i + 1)],
-                    in0=accs[i][:],
-                    in1=bias[u % SLOTS][:, BLK * half : BLK * (half + 1)],
-                    op=ADD,
-                )
+            raw = work.tile([P, UNIT], F32, name="raw", bufs=6)
+            for i in range(len(halves)):
+                nc.scalar.copy(out=raw[:, BLK * i : BLK * (i + 1)], in_=accs[i][:])
+            col = unit_col0(u) + halves[0] * BLK
+            width = BLK * len(halves)
+            nc.vector.tensor_tensor(out=dst[:, 0:width], in0=raw[:, 0:width], in1=bias[:, col : col + width], op=ADD)
 
         def store(res, u, halves, m):
             part, a = units[u]
             c0 = a * UNIT + halves[0] * BLK
             width = BLK * len(halves)
-            nc.scalar.dma_start(out=outs[part][P * m : P * (m + 1), c0 : c0 + width], in_=res[:, 0:width])
+            nc.sync.dma_start(out=outs[part][P * m : P * (m + 1), c0 : c0 + width], in_=res[:, 0:width])
 
         def products(y, m):
             yc = work.tile([P, 8, 128], F32, name="yc")
@@ -159,6 +158,8 @@ def tile_flashneoxattention_pa_kernel(
 
         warm = keep.tile([P, BLK], BF16, name="warm")
         nc.gpsimd.memset(warm[:], 0.0)
+        table = keep.tile([P, 8], BF16, name="table")
+        nc.scalar.copy(out=table[:], in_=warm[:, 0:8])
         warm_acc = psum.tile([P, BLK], F32, name="acc%d" % (BANKS - 1))
         for i in range(WARM_MATMULS):
             nc.tensor.matmul(out=warm_acc[:], lhsT=warm[:, 0:P], rhs=warm[:], start=True, stop=True)
@@ -189,8 +190,8 @@ def tile_flashneoxattention_pa_kernel(
         load_bias(0)
         load_w_scales(1, 0, PASSES)
         load_w_codes(1, 0, PASSES)
-        nc.gpsimd.dma_start(out=cos_sb[:], in_=cos.rearrange("(m p) d -> p m d", p=P))
-        nc.gpsimd.dma_start(out=sin_sb[:], in_=sin.rearrange("(m p) d -> p m d", p=P))
+        nc.sync.dma_start(out=cos_sb[:], in_=cos.rearrange("(m p) d -> p m d", p=P))
+        nc.sync.dma_start(out=sin_sb[:], in_=sin.rearrange("(m p) d -> p m d", p=P))
         load_bias(1)
         load_unit(2)
 
@@ -244,9 +245,9 @@ def tile_flashneoxattention_pa_kernel(
             for g in range(PASSES):
                 multiply(acc, u, halves[0], m, g, c0, BLK // 2)
             res = work.tile([P, UNIT], F32, name="res", bufs=6)
-            col = halves[0] * BLK + c0
+            col = unit_col0(u) + halves[0] * BLK + c0
             nc.vector.tensor_tensor(
-                out=res[:, 0 : BLK // 2], in0=acc[:, 0 : BLK // 2], in1=bias[u % SLOTS][:, col : col + BLK // 2], op=ADD
+                out=res[:, 0 : BLK // 2], in0=acc[:, 0 : BLK // 2], in1=bias[:, col : col + BLK // 2], op=ADD
             )
             oc = units[u][1] * UNIT + halves[0] * BLK + c0
             queue.dma_start(out=outs[V_PART][P * m : P * (m + 1), oc : oc + BLK // 2], in_=res[:, 0 : BLK // 2])

@@ -187,9 +187,9 @@ def tile_flashneoxattention_pa_kernel(
         load_w_codes(0, 4, 6)
         load_x_codes(6, PASSES)
         load_w_codes(0, 6, PASSES)
-        load_bias(0)
         load_w_scales(1, 0, PASSES)
         load_w_codes(1, 0, PASSES)
+        load_bias(0)
         nc.sync.dma_start(out=cos_sb[:], in_=cos.rearrange("(m p) d -> p m d", p=P))
         nc.sync.dma_start(out=sin_sb[:], in_=sin.rearrange("(m p) d -> p m d", p=P))
         load_bias(1)

from contextlib import ExitStack

import concourse.mybir as mybir

FLOPS = 2 * 512 * 4096 * 12288

F32 = mybir.dt.float32
BF16 = mybir.dt.bfloat16
U8 = mybir.dt.uint8
I32 = mybir.dt.int32
FP4X4 = mybir.dt.float4_e2m1fn_x4
ADD = mybir.AluOpType.add
SUB = mybir.AluOpType.subtract
MULT = mybir.AluOpType.mult

P = 128
PASSES = 8
TOK_TILES = 4
BLK = 512
UNIT = 1024
SLOTS = 4
BANKS = 8
WARM_MATMULS = 12
PART_COLS = 4096
Q_PART, K_PART, V_PART = 0, 1, 2


def tile_flashneoxattention_pa_kernel(
    tc, x_words, x_scales, cos, sin, w_words, w_scales, b_qkv, out_q, out_k, out_v
):
    nc = tc.nc
    outs = [o.rearrange("t h d -> t (h d)") for o in (out_q, out_k, out_v)]

    units = []
    for a in range(4):
        units.extend([(V_PART, a), (Q_PART, a), (K_PART, a)])

    steps = [(u, (0, 1)) for u in range(1, 9)] + [(9, (0,)), (10, (0, 1)), (11, (0, 1)), (9, (1,))]

    with ExitStack() as ctx:
        keep = ctx.enter_context(tc.tile_pool(name="keep", bufs=1))
        work = ctx.enter_context(tc.tile_pool(name="work", bufs=2))
        psum = ctx.enter_context(tc.psum_pool(name="psum", bufs=1))
        ctx.enter_context(tc.manual_schedule())

        x_codes = keep.tile([P, PASSES, 2 * 512], U8, name="x_codes", align_bytes=64)
        x_planes = keep.tile([P, PASSES, 512], U8, name="x_planes", align_bytes=64)
        w_codes = [keep.tile([P, PASSES, 2 * UNIT], U8, name="w_codes%d" % s, align_bytes=64) for s in range(SLOTS)]
        w_planes = [keep.tile([P, PASSES, UNIT], U8, name="w_planes%d" % s, align_bytes=64) for s in range(SLOTS)]
        bias = keep.tile([P, 3 * PART_COLS], BF16, name="bias")
        cos_sb = keep.tile([P, TOK_TILES, 128], BF16, name="cos_sb")
        sin_sb = keep.tile([P, TOK_TILES, 128], BF16, name="sin_sb")

        def unit_col0(u):
            return units[u][0] * PART_COLS + units[u][1] * UNIT

        def zero(plane, g0, g1):
            nc.vector.memset(plane[:, g0:g1, :].bitcast(I32), 0)

        def load_x_codes(g0, g1):
            nc.sync.dma_start(
                out=x_codes[:, g0:g1, :].bitcast(I32),
                in_=x_words[g0:g1].rearrange("g p b -> p g b").bitcast(I32),
            )

        def load_x_scales(g0, g1):
            for quad in range(4):
                nc.sync.dma_start(
                    out=x_planes[32 * quad : 32 * quad + 4, g0:g1, :].bitcast(I32),
                    in_=x_scales[g0:g1, 4 * quad : 4 * quad + 4, :].rearrange("g r n -> r g n").bitcast(I32),
                )

        def load_w_codes(u, g0, g1):
            col = unit_col0(u)
            nc.sync.dma_start(
                out=w_codes[u % SLOTS][:, g0:g1, :].bitcast(I32),
                in_=w_words[g0:g1, :, 2 * col : 2 * (col + UNIT)].rearrange("g p b -> p g b").bitcast(I32),
            )

        def load_w_scales(u, g0, g1):
            col = unit_col0(u)
            for quad in range(4):
                nc.sync.dma_start(
                    out=w_planes[u % SLOTS][32 * quad : 32 * quad + 4, g0:g1, :].bitcast(I32),
                    in_=w_scales[g0:g1, 4 * quad : 4 * quad + 4, col : col + UNIT]
                    .rearrange("g r n -> r g n")
                    .bitcast(I32),
                )

        def load_bias(u):
            col = unit_col0(u)
            nc.sync.dma_start(out=bias[:, col : col + UNIT], in_=b_qkv[col : col + UNIT].partition_broadcast(P))

        def load_unit(u):
            load_w_scales(u, 0, PASSES)
            load_w_codes(u, 0, PASSES)
            load_bias(u)

        bank_count = [0]

        def new_bank():
            n = bank_count[0]
            bank_count[0] = n + 1
            return psum.tile([P, BLK], F32, name="acc%d" % (n % BANKS))

        def multiply(acc, u, half, m, g, c0=0, width=BLK):
            slot = u % SLOTS
            lo = BLK * half + c0
            nc.tensor.matmul_mx(
                out=acc[:, 0:width],
                lhsT=x_codes[:, g, 256 * m : 256 * (m + 1)].bitcast(FP4X4),
                lhsT_scale=x_planes[:, g, 128 * m : 128 * (m + 1)],
                rhs=w_codes[slot][:, g, 2 * lo : 2 * (lo + width)].bitcast(FP4X4),
                rhs_scale=w_planes[slot][:, g, lo : lo + width],
                start=(g == 0),
                stop=(g == PASSES - 1),
            )

        def add_bias(dst, accs, u, halves):
            raw = work.tile([P, UNIT], F32, name="raw", bufs=6)
            for i in range(len(halves)):
                nc.scalar.copy(out=raw[:, BLK * i : BLK * (i + 1)], in_=accs[i][:])
            col = unit_col0(u) + halves[0] * BLK
            width = BLK * len(halves)
            nc.vector.tensor_tensor(out=dst[:, 0:width], in0=raw[:, 0:width], in1=bias[:, col : col + width], op=ADD)

        def store(res, u, halves, m):
            part, a = units[u]
            c0 = a * UNIT + halves[0] * BLK
            width = BLK * len(halves)
            nc.sync.dma_start(out=outs[part][P * m : P * (m + 1), c0 : c0 + width], in_=res[:, 0:width])

        def products(y, m):
            yc = work.tile([P, 8, 128], F32, name="yc")
            ys = work.tile([P, 8, 128], F32, name="ys")
            y3 = y[:].rearrange("p (a d) -> p a d", d=128)
            nc.vector.tensor_tensor(
                out=yc[:], in0=y3, in1=cos_sb[:, m, :].unsqueeze(1).to_broadcast([P, 8, 128]), op=MULT
            )
            nc.vector.tensor_tensor(
                out=ys[:], in0=y3, in1=sin_sb[:, m, :].unsqueeze(1).to_broadcast([P, 8, 128]), op=MULT
            )
            return yc, ys

        def combine(yc, ys, u, halves, m):
            res = work.tile([P, UNIT], F32, name="res", bufs=6)
            r4 = res[:].rearrange("p (h j d) -> p h j d", j=2, d=128)
            c4 = yc[:].rearrange("p (h j) d -> p h j d", j=2)
            s4 = ys[:].rearrange("p (h j) d -> p h j d", j=2)
            nc.vector.tensor_tensor(out=r4[:, :, 0, :], in0=c4[:, :, 0, :], in1=s4[:, :, 1, :], op=SUB)
            nc.vector.tensor_tensor(out=r4[:, :, 1, :], in0=c4[:, :, 1, :], in1=s4[:, :, 0, :], op=ADD)
            store(res, u, halves, m)

        def value_rows(accs, u, halves, m):
            res = work.tile([P, UNIT], F32, name="res", bufs=6)
            add_bias(res, accs, u, halves)
            store(res, u, halves, m)

        warm = keep.tile([P, BLK], BF16, name="warm")
        nc.gpsimd.memset(warm[:], 0.0)
        table = keep.tile([P, 8], BF16, name="table")
        nc.scalar.copy(out=table[:], in_=warm[:, 0:8])
        warm_acc = psum.tile([P, BLK], F32, name="acc%d" % (BANKS - 1))
        for i in range(WARM_MATMULS):
            nc.tensor.matmul(out=warm_acc[:], lhsT=warm[:, 0:P], rhs=warm[:], start=True, stop=True)

        zero(x_planes, 0, 2)
        zero(w_planes[0], 0, 2)
        zero(x_planes, 2, PASSES)
        zero(w_planes[0], 2, PASSES)
        zero(w_planes[1], 0, PASSES)
        zero(w_planes[2], 0, PASSES)

        load_x_codes(0, 1)
        load_w_codes(0, 0, 1)
        load_x_scales(0, 2)
        load_w_scales(0, 0, 2)
        load_x_codes(1, 2)
        load_w_codes(0, 1, 2)
        load_x_scales(2, 4)
        load_w_scales(0, 2, 4)
        load_x_codes(2, 4)
        load_w_codes(0, 2, 4)
        load_x_scales(4, PASSES)
        load_w_scales(0, 4, PASSES)
        load_x_codes(4, 6)
        load_w_codes(0, 4, 6)
        load_x_codes(6, PASSES)
        load_w_codes(0, 6, PASSES)
        load_w_scales(1, 0, PASSES)
        load_w_codes(1, 0, PASSES)
        load_bias(0)
        nc.sync.dma_start(out=cos_sb[:], in_=cos.rearrange("(m p) d -> p m d", p=P))
        nc.sync.dma_start(out=sin_sb[:], in_=sin.rearrange("(m p) d -> p m d", p=P))
        load_bias(1)
        load_unit(2)

        head = [new_bank() for i in range(BANKS)]
        for g in range(PASSES):
            for m in range(TOK_TILES):
                for half in range(2):
                    multiply(head[2 * m + half], 0, half, m, g)
        for m in range(TOK_TILES):
            value_rows(head[2 * m : 2 * m + 2], 0, (0, 1), m)
        zero(w_planes[3], 0, PASSES)
        load_unit(3)
        load_unit(4)
        next_unit = 5
        halves_left = [2] * len(units)
        halves_left[0] = 0

        pending = None
        for u, halves in steps:
            last_step = (u, halves) == steps[-1]
            for m in range(TOK_TILES):
                if last_step and m == TOK_TILES - 1:
                    break
                accs = []
                for half in halves:
                    acc = new_bank()
                    for g in range(PASSES):
                        multiply(acc, u, half, m, g)
                    accs.append(acc)
                if units[u][0] == V_PART:
                    value_rows(accs, u, halves, m)
                    if pending is not None:
                        combine(*pending)
                        pending = None
                else:
                    y = work.tile([P, UNIT], F32, name="y")
                    add_bias(y, accs, u, halves)
                    if pending is not None:
                        combine(*pending)
                    yc, ys = products(y, m)
                    pending = (yc, ys, u, halves, m)
            halves_left[u] -= len(halves)
            while next_unit < len(units) and halves_left[next_unit - SLOTS] == 0:
                load_unit(next_unit)
                next_unit += 1
        u, halves = steps[-1]
        m = TOK_TILES - 1
        for i, queue in enumerate((nc.scalar, nc.sync)):
            c0 = i * (BLK // 2)
            acc = new_bank()
            for g in range(PASSES):
                multiply(acc, u, halves[0], m, g, c0, BLK // 2)
            res = work.tile([P, UNIT], F32, name="res", bufs=6)
            col = unit_col0(u) + halves[0] * BLK + c0
            nc.vector.tensor_tensor(
                out=res[:, 0 : BLK // 2], in0=acc[:, 0 : BLK // 2], in1=bias[:, col : col + BLK // 2], op=ADD
            )
            oc = units[u][1] * UNIT + halves[0] * BLK + c0
            queue.dma_start(out=outs[V_PART][P * m : P * (m + 1), oc : oc + BLK // 2], in_=res[:, 0 : BLK // 2])
